import numpy as np
import ml_dtypes


BF16 = ml_dtypes.bfloat16


def bf(x):
    return np.asarray(x, np.float32).astype(BF16)


def f64(x):
    return np.asarray(x).astype(np.float64)


E2M1 = np.array([0.0, 0.5, 1.0, 1.5, 2.0, 3.0, 4.0, 6.0, -0.0, -0.5, -1.0, -1.5, -2.0, -3.0, -4.0, -6.0])


def pack_weight(w, fmt):
    k, n = w.shape
    w = f64(bf(w)).reshape(k // 32, 32, n)
    amax = np.abs(w).max(1)
    if fmt == "e4m3":
        byte = np.frexp(amax)[1] - 1 + 127 - 7
    else:
        mant, ex = np.frexp(amax / 6.0)
        byte = np.where(mant > 0.5, ex, ex - 1) + 127
    byte = np.clip(np.where(amax > 0, byte, 1), 1, 254)
    scaled = (w * np.exp2(127.0 - byte)[:, None, :]).reshape(k, n).astype(np.float32)
    by_word = np.ascontiguousarray(scaled.reshape(k // 512, 128, 4, n).transpose(0, 1, 3, 2))
    if fmt == "e4m3":
        words = by_word.astype(ml_dtypes.float8_e4m3fn).view(np.uint8)
    else:
        c = by_word.astype(ml_dtypes.float4_e2m1fn).view(np.uint8) & 0xF
        words = c[..., 0::2] | (c[..., 1::2] << 4)
    return np.ascontiguousarray(words), np.ascontiguousarray(byte.astype(np.uint8).reshape(k // 512, 16, n))


def unpack_weight(words, scales, fmt):
    g, p, n, _ = words.shape
    if fmt == "e4m3":
        vals = np.ascontiguousarray(words).view(ml_dtypes.float8_e4m3fn).astype(np.float64)
    else:
        nib = np.empty((g, p, n, 4), np.uint8)
        nib[..., 0::2] = words & 0xF
        nib[..., 1::2] = words >> 4
        vals = E2M1[nib]
    vals = vals * np.repeat(np.exp2(scales.astype(np.float64) - 127.0), 8, axis=1)[..., None]
    return vals.transpose(0, 1, 3, 2).reshape(g * 512, n)

def pack4(w):
    words, scales = pack_weight(w, "e2m1")
    return words.reshape(words.shape[0], 128, -1), scales


def unpack4(words, scales):
    return unpack_weight(words.reshape(words.shape[0], 128, -1, 2), scales, "e2m1")


def kspread(k):
    return np.exp2(np.repeat(np.random.randint(-6, 7, k // 32), 32).astype(np.float64))


B, T, D, H, KV, DH = 2, 1024, 4096, 16, 4, 128
G = H // KV
HALF = DH // 2
ROPE_THETA = 1e6
YARN_FACTOR = 64.0
ORIG_MAX_POS = 4096.0
BETA_FAST, BETA_SLOW = 4.0, 1.0
ATTN_FACTOR = 0.1 * np.log(YARN_FACTOR) + 1.0


def corr_dim(num_rot):
    return DH * np.log(ORIG_MAX_POS / (num_rot * 2 * np.pi)) / (2 * np.log(ROPE_THETA))


def yarn_inv_freq():
    low = float(np.sum(np.arange(DH) + 1 <= corr_dim(BETA_FAST)))
    high = min(float(np.sum(np.arange(DH) < corr_dim(BETA_SLOW))), DH - 1.0)
    if low == high:
        high += 0.001
    ramp = np.clip((np.arange(HALF) - low) / (high - low), 0.0, 1.0)
    pos_freqs = ROPE_THETA ** (np.arange(0, DH, 2) / DH)
    inv_extrap = 1.0 / pos_freqs
    inv_interp = 1.0 / (YARN_FACTOR * pos_freqs)
    extrap_factor = 1.0 - ramp
    return inv_interp * (1.0 - extrap_factor) + inv_extrap * extrap_factor


def rope_yarn(v):
    angles = np.arange(T)[:, None] * yarn_inv_freq()[None, :]
    cos = np.cos(angles)[None, :, None, :]
    sin = np.sin(angles)[None, :, None, :]
    v_even = v[..., 0::2]
    v_odd = v[..., 1::2]
    out_even = v_even * cos - v_odd * sin
    out_odd = v_even * sin + v_odd * cos
    return np.stack([out_even, out_odd], axis=-1).reshape(v.shape) * ATTN_FACTOR


def setup_inputs():
    s = kspread(D)
    x = np.random.standard_normal((B, T, D)) * s
    x_words, x_scales = pack4(x.reshape(B * T, D).T)
    words, scales = pack4(np.random.standard_normal((D, (H + 2 * KV) * DH)) / np.sqrt(D) / s[:, None])
    return {"x_words": x_words, "x_scales": x_scales, "w_qkv_words": words, "w_qkv_scales": scales}


def reference(x_words, x_scales, w_qkv_words, w_qkv_scales):
    qkv = unpack4(x_words, x_scales).T.reshape(B, T, D) @ unpack4(w_qkv_words, w_qkv_scales)
    q = qkv[:, :, :H * DH].reshape(B, T, H, DH)
    k = qkv[:, :, H * DH:(H + KV) * DH].reshape(B, T, KV, DH)
    v = qkv[:, :, (H + KV) * DH:].reshape(B, T, KV, DH)
    q = rope_yarn(q)
    k = rope_yarn(k)
    q = q.reshape(B, T, KV, G, DH).transpose(0, 2, 3, 1, 4)
    k = k.transpose(0, 2, 1, 3)
    v = v.transpose(0, 2, 1, 3)
    return q, k, v

@@ -1,0 +1,291 @@
+import math
+from contextlib import ExitStack
+
+import concourse.mybir as mybir
+
+F32 = mybir.dt.float32
+BF16 = mybir.dt.bfloat16
+I32 = mybir.dt.int32
+U8 = mybir.dt.uint8
+FP4X4 = mybir.dt.float4_e2m1fn_x4
+ALU = mybir.AluOpType
+ACT = mybir.ActivationFunctionType
+
+P = 128
+BATCH, SEQ, FEATURES = 2, 1024, 4096
+HEAD_DIM = 128
+HALF_DIM = HEAD_DIM // 2
+CHANNELS = 3072
+PASSES = FEATURES // 512
+TILES = SEQ // P
+COLS = 512
+BLOCKS = CHANNELS // COLS
+HEADS = COLS // HEAD_DIM
+KEY_BLOCK, VALUE_BLOCK = 4, 5
+EARLY = 4
+
+ROPE_BASE = 1e6
+YARN_FACTOR = 64.0
+ROPE_SCALE = 0.1 * math.log(YARN_FACTOR) + 1.0
+RAMP_LOW, RAMP_WIDTH = 23.0, 8.0
+
+FLOPS = 2 * BATCH * SEQ * FEATURES * CHANNELS
+
+
+def tile_causalselfattentiongqa_pa_kernel(
+    tc, x_words, x_scales, w_words, w_scales, out_q, out_k, out_v
+):
+    nc = tc.nc
+    with ExitStack() as ctx:
+        keep = ctx.enter_context(tc.tile_pool(name="keep", bufs=1))
+        work = ctx.enter_context(tc.tile_pool(name="work", bufs=3))
+        results = ctx.enter_context(tc.tile_pool(name="results", bufs=12))
+        psum = ctx.enter_context(tc.psum_pool(name="psum", bufs=8))
+        ctx.enter_context(tc.manual_schedule())
+
+        def codes_tile(name, passes, cols):
+            return keep.tile([P, passes, 2 * cols], U8, name=name, align_bytes=256)
+
+        def plane_tile(name, passes, cols, engine):
+            plane = keep.tile([P, passes, cols], U8, name=name, align_bytes=256)
+            engine.memset(plane[:].rearrange("p g n -> p (g n)").bitcast(I32), 0)
+            return plane
+
+        def load_codes(tile, words, g0, g1, c0, c1):
+            nc.sync.dma_start(
+                out=tile[:].bitcast(I32),
+                in_=words[g0:g1, :, 2 * c0 : 2 * c1].rearrange("g p n -> p g n").bitcast(I32),
+            )
+
+        def load_scales(plane, scales, g0, g1, c0, c1):
+            for q in range(4):
+                nc.sync.dma_start(
+                    out=plane[32 * q : 32 * q + 4, :, :].bitcast(I32),
+                    in_=scales[g0:g1, 4 * q : 4 * q + 4, c0:c1].rearrange("g r n -> r g n").bitcast(I32),
+                )
+
+        idle = keep.tile([P, P + COLS], BF16, name="idle")
+        nc.vector.memset(idle[:], 0.0)
+        SCALE_RUNS = ((0, 2), (2, 5), (5, 8))
+        CODE_RUNS = ((0, 1), (1, 2), (2, 4), (4, 6), (6, 8))
+
+        index = keep.tile([P, HALF_DIM], F32, name="index")
+        nc.gpsimd.iota(index[:], pattern=[[1, HALF_DIM]], base=0, channel_multiplier=0, allow_small_or_imprecise_dtypes=True)
+        position = keep.tile([P, TILES], F32, name="position")
+        nc.gpsimd.iota(position[:], pattern=[[P, TILES]], base=0, channel_multiplier=1, allow_small_or_imprecise_dtypes=True)
+
+        xs0, ws0 = [], []
+        for i, (g0, g1) in enumerate(SCALE_RUNS):
+            engine = nc.vector if i == 0 else nc.gpsimd
+            xs0.append(plane_tile("xs0_%d" % i, g1 - g0, SEQ, engine))
+            ws0.append(plane_tile("ws0_%d" % i, g1 - g0, COLS, engine))
+        ws = [None] + [plane_tile("ws%d" % c, PASSES, COLS, nc.gpsimd) for c in range(1, BLOCKS)]
+        xs1 = plane_tile("xs1", PASSES, SEQ, nc.gpsimd)
+
+        xc0 = [codes_tile("xc0_%d" % i, g1 - g0, SEQ) for i, (g0, g1) in enumerate(CODE_RUNS)]
+        wc0 = [codes_tile("wc0_%d" % i, g1 - g0, COLS) for i, (g0, g1) in enumerate(CODE_RUNS)]
+        wc = [None] + [codes_tile("wc%d" % c, PASSES, COLS) for c in range(1, BLOCKS)]
+        xc1 = codes_tile("xc1", PASSES, SEQ)
+
+        def codes0(i):
+            g0, g1 = CODE_RUNS[i]
+            load_codes(xc0[i], x_words, g0, g1, 0, SEQ)
+            load_codes(wc0[i], w_words, g0, g1, 0, COLS)
+
+        def scales0(i):
+            g0, g1 = SCALE_RUNS[i]
+            load_scales(xs0[i], x_scales, g0, g1, 0, SEQ)
+            load_scales(ws0[i], w_scales, g0, g1, 0, COLS)
+
+        codes0(0)
+        scales0(0)
+        codes0(1)
+        scales0(1)
+        codes0(2)
+        scales0(2)
+        codes0(3)
+        codes0(4)
+        for c in range(1, BLOCKS):
+            load_scales(ws[c], w_scales, 0, PASSES, c * COLS, (c + 1) * COLS)
+            load_codes(wc[c], w_words, 0, PASSES, c * COLS, (c + 1) * COLS)
+        load_scales(xs1, x_scales, 0, PASSES, SEQ, 2 * SEQ)
+        load_codes(xc1, x_words, 0, PASSES, SEQ, 2 * SEQ)
+
+        freq = keep.tile([P, HALF_DIM], F32, name="freq")
+        nc.vector.memset(freq[:, 0:1], 1.0)
+        n = 1
+        while n < HALF_DIM:
+            nc.vector.tensor_scalar(
+                freq[:, n : 2 * n], freq[:, 0:n], ROPE_BASE ** (-n / HALF_DIM), None, ALU.mult
+            )
+            n *= 2
+        ramp = keep.tile([P, HALF_DIM], F32, name="ramp")
+        nc.vector.tensor_scalar(ramp[:], index[:], -RAMP_LOW, 1.0 / RAMP_WIDTH, ALU.add, ALU.mult)
+        nc.vector.tensor_scalar(ramp[:], ramp[:], 0.0, 1.0, ALU.max, ALU.min)
+        nc.vector.tensor_scalar(ramp[:], ramp[:], 1.0 / YARN_FACTOR - 1.0, 1.0, ALU.mult, ALU.add)
+        nc.vector.tensor_tensor(freq[:], freq[:], ramp[:], ALU.mult)
+
+        angle = keep.tile([P, TILES, HALF_DIM], F32, name="angle")
+        nc.vector.tensor_tensor(
+            angle[:],
+            freq[:].unsqueeze(1).to_broadcast([P, TILES, HALF_DIM]),
+            position[:].unsqueeze(2).to_broadcast([P, TILES, HALF_DIM]),
+            ALU.mult,
+        )
+        turns = keep.tile([P, TILES, HALF_DIM], I32, name="turns")
+        nc.vector.tensor_scalar(turns[:], angle[:], 0.5 / math.pi, None, ALU.mult)
+        rest = keep.tile([P, TILES * HALF_DIM], F32, name="rest")
+        nc.vector.scalar_tensor_tensor(
+            rest[:],
+            turns[:].rearrange("p t i -> p (t i)"),
+            -2.0 * math.pi,
+            angle[:].rearrange("p t i -> p (t i)"),
+            ALU.mult,
+            ALU.add,
+        )
+        pairs = [P, TILES * HALF_DIM, 2]
+        sign = keep.tile([P, 2], F32, name="sign")
+        nc.vector.memset(sign[:, 0:1], 1.0)
+        nc.vector.memset(sign[:, 1:2], -1.0)
+        sin_raw = keep.tile(pairs, F32, name="sin_raw")
+        nc.scalar.activation(sin_raw[:], rest[:].unsqueeze(2).to_broadcast(pairs), ACT.Sin)
+        size = keep.tile([P, TILES * HALF_DIM], F32, name="size")
+        nc.scalar.activation(size[:], rest[:], ACT.Abs)
+        cos_raw = keep.tile(pairs, F32, name="cos_raw")
+        nc.scalar.activation(
+            cos_raw[:], size[:].unsqueeze(2).to_broadcast(pairs), ACT.Sin, bias=0.5 * math.pi, scale=-1.0
+        )
+        sin_table = keep.tile([P, TILES, HEAD_DIM], F32, name="sin_table")
+        nc.vector.scalar_tensor_tensor(
+            sin_table[:].rearrange("p t (i j) -> p (t i) j", j=2),
+            sin_raw[:],
+            ROPE_SCALE,
+            sign[:].unsqueeze(1).to_broadcast(pairs),
+            ALU.mult,
+            ALU.mult,
+        )
+        cos_table = keep.tile([P, TILES, HEAD_DIM], F32, name="cos_table")
+        nc.vector.tensor_scalar(
+            cos_table[:].rearrange("p t d -> p (t d)"),
+            cos_raw[:].rearrange("p a j -> p (a j)"),
+            ROPE_SCALE,
+            None,
+            ALU.mult,
+        )
+
+        warm = psum.tile([P, COLS], F32, name="bank")
+        for i in range(12):
+            nc.tensor.matmul(warm[:], lhsT=idle[:, 0:P], rhs=idle[:, P : P + COLS], start=True, stop=True)
+
+        def run_of(runs, g):
+            for i, (g0, g1) in enumerate(runs):
+                if g0 <= g < g1:
+                    return i, g - g0
+
+        def x_operand(half, g, t):
+            a = t * P
+            if half == 1:
+                return xc1[:, g, 2 * a : 2 * (a + P)].bitcast(FP4X4), xs1[:, g, a : a + P]
+            i, u = run_of(CODE_RUNS, g)
+            j, v = run_of(SCALE_RUNS, g)
+            return xc0[i][:, u, 2 * a : 2 * (a + P)].bitcast(FP4X4), xs0[j][:, v, a : a + P]
+
+        def w_operand(c, g, n0, n1):
+            if c > 0:
+                return wc[c][:, g, 2 * n0 : 2 * n1].bitcast(FP4X4), ws[c][:, g, n0:n1]
+            i, u = run_of(CODE_RUNS, g)
+            j, v = run_of(SCALE_RUNS, g)
+            return wc0[i][:, u, 2 * n0 : 2 * n1].bitcast(FP4X4), ws0[j][:, v, n0:n1]
+
+        def multiply(bank, half, c, t, g, n0=0, n1=COLS):
+            x_codes, x_plane = x_operand(half, g, t)
+            w_codes, w_plane = w_operand(c, g, n0, n1)
+            nc.tensor.matmul_mx(
+                out=bank[:, 0 : n1 - n0],
+                lhsT=x_codes,
+                lhsT_scale=x_plane,
+                rhs=w_codes,
+                rhs_scale=w_plane,
+                start=(g == 0),
+                stop=(g == PASSES - 1),
+            )
+
+        def home(half, c, t):
+            rows = slice(t * P, (t + 1) * P)
+            if c == VALUE_BLOCK:
+                view = out_v[half, :, rows, :]
+            elif c == KEY_BLOCK:
+                view = out_k[half, :, rows, :]
+            else:
+                view = out_q[half, c, :, rows, :]
+            return view.rearrange("h p d -> p h d")
+
+        by_head = [P, HEADS, HEAD_DIM]
+        waiting = []
+
+        def finish_rope():
+            for half, c, t, straight, crossed in waiting:
+                result = results.tile([P, HEADS, HEAD_DIM], F32, name="result")
+                nc.vector.tensor_tensor(
+                    result[:].rearrange("p h (i j) -> p (h i) j", j=2),
+                    straight[:].rearrange("p h (i j) -> p (h i) j", j=2),
+                    crossed[:].rearrange("p h (i j) -> p (h i) j", j=2)[:, :, ::-1],
+                    ALU.add,
+                )
+                nc.sync.dma_start(out=home(half, c, t), in_=result[:])
+            waiting.clear()
+
+        def epilogue(bank, half, c, t):
+            values = bank[:].rearrange("p (h d) -> p h d", h=HEADS)
+            if c == VALUE_BLOCK:
+                finish_rope()
+                result = results.tile([P, HEADS, HEAD_DIM], F32, name="result")
+                nc.scalar.copy(result[:], values)
+                nc.sync.dma_start(out=home(half, c, t), in_=result[:])
+                return
+            straight = work.tile([P, HEADS, HEAD_DIM], F32, name="straight")
+            crossed = work.tile([P, HEADS, HEAD_DIM], F32, name="crossed")
+            nc.vector.tensor_tensor(
+                straight[:], values, cos_table[:, t, :].unsqueeze(1).to_broadcast(by_head), ALU.mult
+            )
+            nc.vector.tensor_tensor(
+                crossed[:], values, sin_table[:, t, :].unsqueeze(1).to_broadcast(by_head), ALU.mult
+            )
+            finish_rope()
+            waiting.append((half, c, t, straight, crossed))
+
+        banks = []
+        for t in range(TILES):
+            bank = psum.tile([P, COLS], F32, name="bank")
+            banks.append(bank)
+        for g in range(EARLY):
+            for t in range(TILES):
+                multiply(banks[t], 0, 0, t, g)
+        for t in range(TILES):
+            for g in range(EARLY, PASSES):
+                multiply(banks[t], 0, 0, t, g)
+            epilogue(banks[t], 0, 0, t)
+
+        for half in range(BATCH):
+            for c in range(1 if half == 0 else 0, BLOCKS):
+                for t in range(TILES):
+                    if half == BATCH - 1 and c == BLOCKS - 1 and t == TILES - 1:
+                        continue
+                    bank = psum.tile([P, COLS], F32, name="bank")
+                    for g in range(PASSES):
+                        multiply(bank, half, c, t, g)
+                    epilogue(bank, half, c, t)
+
+        half, c, t = BATCH - 1, BLOCKS - 1, TILES - 1
+        for part in range(2):
+            n0, n1 = part * COLS // 2, (part + 1) * COLS // 2
+            bank = psum.tile([P, COLS], F32, name="bank")
+            for g in range(PASSES):
+                multiply(bank, half, c, t, g, n0, n1)
+            result = results.tile([P, HEADS // 2, HEAD_DIM], F32, name="result_part")
+            values = bank[:, 0 : COLS // 2].rearrange("p (h d) -> p h d", d=HEAD_DIM)
+            if part == 0:
+                nc.scalar.copy(result[:], values)
+            else:
+                nc.vector.tensor_copy(result[:], values)
+            nc.sync.dma_start(out=home(half, c, t)[:, part * HEADS // 2 : (part + 1) * HEADS // 2, :], in_=result[:])

@@ -65,7 +65,7 @@ def tile_causalselfattentiongqa_pa_kernel(
                 )
 
         idle = keep.tile([P, P + COLS], BF16, name="idle")
-        nc.vector.memset(idle[:], 0.0)
+        nc.gpsimd.memset(idle[:].bitcast(I32), 0)
         SCALE_RUNS = ((0, 2), (2, 5), (5, 8))
         CODE_RUNS = ((0, 1), (1, 2), (2, 4), (4, 6), (6, 8))
 
@@ -82,10 +82,11 @@ def tile_causalselfattentiongqa_pa_kernel(
         ws = [None] + [plane_tile("ws%d" % c, PASSES, COLS, nc.gpsimd) for c in range(1, BLOCKS)]
         xs1 = plane_tile("xs1", PASSES, SEQ, nc.gpsimd)
 
-        xc0 = [codes_tile("xc0_%d" % i, g1 - g0, SEQ) for i, (g0, g1) in enumerate(CODE_RUNS)]
+        xc0 = [codes_tile("xc0_%d" % i, g1 - g0, SEQ - P if i == 0 else SEQ) for i, (g0, g1) in enumerate(CODE_RUNS)]
         wc0 = [codes_tile("wc0_%d" % i, g1 - g0, COLS) for i, (g0, g1) in enumerate(CODE_RUNS)]
         wc = [None] + [codes_tile("wc%d" % c, PASSES, COLS) for c in range(1, BLOCKS)]
         xc1 = codes_tile("xc1", PASSES, SEQ)
+        xc_first = codes_tile("xc_first", 1, P)
 
         def codes0(i):
             g0, g1 = CODE_RUNS[i]
@@ -97,8 +98,10 @@ def tile_causalselfattentiongqa_pa_kernel(
             load_scales(xs0[i], x_scales, g0, g1, 0, SEQ)
             load_scales(ws0[i], w_scales, g0, g1, 0, COLS)
 
-        codes0(0)
+        load_codes(xc_first, x_words, 0, 1, 0, P)
+        load_codes(wc0[0], w_words, 0, 1, 0, COLS)
         scales0(0)
+        load_codes(xc0[0], x_words, 0, 1, P, SEQ)
         codes0(1)
         scales0(1)
         codes0(2)
@@ -174,7 +177,7 @@ def tile_causalselfattentiongqa_pa_kernel(
         )
 
         warm = psum.tile([P, COLS], F32, name="bank")
-        for i in range(12):
+        for i in range(10):
             nc.tensor.matmul(warm[:], lhsT=idle[:, 0:P], rhs=idle[:, P : P + COLS], start=True, stop=True)
 
         def run_of(runs, g):
@@ -188,7 +191,12 @@ def tile_causalselfattentiongqa_pa_kernel(
                 return xc1[:, g, 2 * a : 2 * (a + P)].bitcast(FP4X4), xs1[:, g, a : a + P]
             i, u = run_of(CODE_RUNS, g)
             j, v = run_of(SCALE_RUNS, g)
-            return xc0[i][:, u, 2 * a : 2 * (a + P)].bitcast(FP4X4), xs0[j][:, v, a : a + P]
+            plane = xs0[j][:, v, a : a + P]
+            if g == 0 and t == 0:
+                return xc_first[:, 0, :].bitcast(FP4X4), plane
+            if g == 0:
+                a -= P
+            return xc0[i][:, u, 2 * a : 2 * (a + P)].bitcast(FP4X4), plane
 
         def w_operand(c, g, n0, n1):
             if c > 0:

import math
from contextlib import ExitStack

import concourse.mybir as mybir

F32 = mybir.dt.float32
BF16 = mybir.dt.bfloat16
I32 = mybir.dt.int32
U8 = mybir.dt.uint8
FP4X4 = mybir.dt.float4_e2m1fn_x4
ALU = mybir.AluOpType
ACT = mybir.ActivationFunctionType

P = 128
BATCH, SEQ, FEATURES = 2, 1024, 4096
HEAD_DIM = 128
HALF_DIM = HEAD_DIM // 2
CHANNELS = 3072
PASSES = FEATURES // 512
TILES = SEQ // P
COLS = 512
BLOCKS = CHANNELS // COLS
HEADS = COLS // HEAD_DIM
KEY_BLOCK, VALUE_BLOCK = 4, 5
EARLY = 4

ROPE_BASE = 1e6
YARN_FACTOR = 64.0
ROPE_SCALE = 0.1 * math.log(YARN_FACTOR) + 1.0
RAMP_LOW, RAMP_WIDTH = 23.0, 8.0

FLOPS = 2 * BATCH * SEQ * FEATURES * CHANNELS


def tile_causalselfattentiongqa_pa_kernel(
    tc, x_words, x_scales, w_words, w_scales, out_q, out_k, out_v
):
    nc = tc.nc
    with ExitStack() as ctx:
        keep = ctx.enter_context(tc.tile_pool(name="keep", bufs=1))
        work = ctx.enter_context(tc.tile_pool(name="work", bufs=3))
        results = ctx.enter_context(tc.tile_pool(name="results", bufs=12))
        psum = ctx.enter_context(tc.psum_pool(name="psum", bufs=8))
        ctx.enter_context(tc.manual_schedule())

        def codes_tile(name, passes, cols):
            return keep.tile([P, passes, 2 * cols], U8, name=name, align_bytes=256)

        def plane_tile(name, passes, cols, engine):
            plane = keep.tile([P, passes, cols], U8, name=name, align_bytes=256)
            engine.memset(plane[:].rearrange("p g n -> p (g n)").bitcast(I32), 0)
            return plane

        def load_codes(tile, words, g0, g1, c0, c1):
            nc.sync.dma_start(
                out=tile[:].bitcast(I32),
                in_=words[g0:g1, :, 2 * c0 : 2 * c1].rearrange("g p n -> p g n").bitcast(I32),
            )

        def load_scales(plane, scales, g0, g1, c0, c1):
            for q in range(4):
                nc.sync.dma_start(
                    out=plane[32 * q : 32 * q + 4, :, :].bitcast(I32),
                    in_=scales[g0:g1, 4 * q : 4 * q + 4, c0:c1].rearrange("g r n -> r g n").bitcast(I32),
                )

        idle = keep.tile([P, P + COLS], BF16, name="idle")
        nc.gpsimd.memset(idle[:].bitcast(I32), 0)
        SCALE_RUNS = ((0, 2), (2, 5), (5, 8))
        CODE_RUNS = ((0, 1), (1, 2), (2, 4), (4, 6), (6, 8))

        index = keep.tile([P, HALF_DIM], F32, name="index")
        nc.gpsimd.iota(index[:], pattern=[[1, HALF_DIM]], base=0, channel_multiplier=0, allow_small_or_imprecise_dtypes=True)
        position = keep.tile([P, TILES], F32, name="position")
        nc.gpsimd.iota(position[:], pattern=[[P, TILES]], base=0, channel_multiplier=1, allow_small_or_imprecise_dtypes=True)

        xs0, ws0 = [], []
        for i, (g0, g1) in enumerate(SCALE_RUNS):
            engine = nc.vector if i == 0 else nc.gpsimd
            xs0.append(plane_tile("xs0_%d" % i, g1 - g0, SEQ, engine))
            ws0.append(plane_tile("ws0_%d" % i, g1 - g0, COLS, engine))
        ws = [None] + [plane_tile("ws%d" % c, PASSES, COLS, nc.gpsimd) for c in range(1, BLOCKS)]
        xs1 = plane_tile("xs1", PASSES, SEQ, nc.gpsimd)

        xc0 = [codes_tile("xc0_%d" % i, g1 - g0, SEQ - P if i == 0 else SEQ) for i, (g0, g1) in enumerate(CODE_RUNS)]
        wc0 = [codes_tile("wc0_%d" % i, g1 - g0, COLS) for i, (g0, g1) in enumerate(CODE_RUNS)]
        wc = [None] + [codes_tile("wc%d" % c, PASSES, COLS) for c in range(1, BLOCKS)]
        xc1 = codes_tile("xc1", PASSES, SEQ)
        xc_first = codes_tile("xc_first", 1, P)

        def codes0(i):
            g0, g1 = CODE_RUNS[i]
            load_codes(xc0[i], x_words, g0, g1, 0, SEQ)
            load_codes(wc0[i], w_words, g0, g1, 0, COLS)

        def scales0(i):
            g0, g1 = SCALE_RUNS[i]
            load_scales(xs0[i], x_scales, g0, g1, 0, SEQ)
            load_scales(ws0[i], w_scales, g0, g1, 0, COLS)

        load_codes(xc_first, x_words, 0, 1, 0, P)
        load_codes(wc0[0], w_words, 0, 1, 0, COLS)
        scales0(0)
        load_codes(xc0[0], x_words, 0, 1, P, SEQ)
        codes0(1)
        scales0(1)
        codes0(2)
        scales0(2)
        codes0(3)
        codes0(4)
        for c in range(1, BLOCKS):
            load_scales(ws[c], w_scales, 0, PASSES, c * COLS, (c + 1) * COLS)
            load_codes(wc[c], w_words, 0, PASSES, c * COLS, (c + 1) * COLS)
        load_scales(xs1, x_scales, 0, PASSES, SEQ, 2 * SEQ)
        load_codes(xc1, x_words, 0, PASSES, SEQ, 2 * SEQ)

        freq = keep.tile([P, HALF_DIM], F32, name="freq")
        nc.vector.memset(freq[:, 0:1], 1.0)
        n = 1
        while n < HALF_DIM:
            nc.vector.tensor_scalar(
                freq[:, n : 2 * n], freq[:, 0:n], ROPE_BASE ** (-n / HALF_DIM), None, ALU.mult
            )
            n *= 2
        ramp = keep.tile([P, HALF_DIM], F32, name="ramp")
        nc.vector.tensor_scalar(ramp[:], index[:], -RAMP_LOW, 1.0 / RAMP_WIDTH, ALU.add, ALU.mult)
        nc.vector.tensor_scalar(ramp[:], ramp[:], 0.0, 1.0, ALU.max, ALU.min)
        nc.vector.tensor_scalar(ramp[:], ramp[:], 1.0 / YARN_FACTOR - 1.0, 1.0, ALU.mult, ALU.add)
        nc.vector.tensor_tensor(freq[:], freq[:], ramp[:], ALU.mult)

        angle = keep.tile([P, TILES, HALF_DIM], F32, name="angle")
        nc.vector.tensor_tensor(
            angle[:],
            freq[:].unsqueeze(1).to_broadcast([P, TILES, HALF_DIM]),
            position[:].unsqueeze(2).to_broadcast([P, TILES, HALF_DIM]),
            ALU.mult,
        )
        turns = keep.tile([P, TILES, HALF_DIM], I32, name="turns")
        nc.vector.tensor_scalar(turns[:], angle[:], 0.5 / math.pi, None, ALU.mult)
        rest = keep.tile([P, TILES * HALF_DIM], F32, name="rest")
        nc.vector.scalar_tensor_tensor(
            rest[:],
            turns[:].rearrange("p t i -> p (t i)"),
            -2.0 * math.pi,
            angle[:].rearrange("p t i -> p (t i)"),
            ALU.mult,
            ALU.add,
        )
        pairs = [P, TILES * HALF_DIM, 2]
        sign = keep.tile([P, 2], F32, name="sign")
        nc.vector.memset(sign[:, 0:1], 1.0)
        nc.vector.memset(sign[:, 1:2], -1.0)
        sin_raw = keep.tile(pairs, F32, name="sin_raw")
        nc.scalar.activation(sin_raw[:], rest[:].unsqueeze(2).to_broadcast(pairs), ACT.Sin)
        size = keep.tile([P, TILES * HALF_DIM], F32, name="size")
        nc.scalar.activation(size[:], rest[:], ACT.Abs)
        cos_raw = keep.tile(pairs, F32, name="cos_raw")
        nc.scalar.activation(
            cos_raw[:], size[:].unsqueeze(2).to_broadcast(pairs), ACT.Sin, bias=0.5 * math.pi, scale=-1.0
        )
        sin_table = keep.tile([P, TILES, HEAD_DIM], F32, name="sin_table")
        nc.vector.scalar_tensor_tensor(
            sin_table[:].rearrange("p t (i j) -> p (t i) j", j=2),
            sin_raw[:],
            ROPE_SCALE,
            sign[:].unsqueeze(1).to_broadcast(pairs),
            ALU.mult,
            ALU.mult,
        )
        cos_table = keep.tile([P, TILES, HEAD_DIM], F32, name="cos_table")
        nc.vector.tensor_scalar(
            cos_table[:].rearrange("p t d -> p (t d)"),
            cos_raw[:].rearrange("p a j -> p (a j)"),
            ROPE_SCALE,
            None,
            ALU.mult,
        )

        warm = psum.tile([P, COLS], F32, name="bank")
        for i in range(10):
            nc.tensor.matmul(warm[:], lhsT=idle[:, 0:P], rhs=idle[:, P : P + COLS], start=True, stop=True)

        def run_of(runs, g):
            for i, (g0, g1) in enumerate(runs):
                if g0 <= g < g1:
                    return i, g - g0

        def x_operand(half, g, t):
            a = t * P
            if half == 1:
                return xc1[:, g, 2 * a : 2 * (a + P)].bitcast(FP4X4), xs1[:, g, a : a + P]
            i, u = run_of(CODE_RUNS, g)
            j, v = run_of(SCALE_RUNS, g)
            plane = xs0[j][:, v, a : a + P]
            if g == 0 and t == 0:
                return xc_first[:, 0, :].bitcast(FP4X4), plane
            if g == 0:
                a -= P
            return xc0[i][:, u, 2 * a : 2 * (a + P)].bitcast(FP4X4), plane

        def w_operand(c, g, n0, n1):
            if c > 0:
                return wc[c][:, g, 2 * n0 : 2 * n1].bitcast(FP4X4), ws[c][:, g, n0:n1]
            i, u = run_of(CODE_RUNS, g)
            j, v = run_of(SCALE_RUNS, g)
            return wc0[i][:, u, 2 * n0 : 2 * n1].bitcast(FP4X4), ws0[j][:, v, n0:n1]

        def multiply(bank, half, c, t, g, n0=0, n1=COLS):
            x_codes, x_plane = x_operand(half, g, t)
            w_codes, w_plane = w_operand(c, g, n0, n1)
            nc.tensor.matmul_mx(
                out=bank[:, 0 : n1 - n0],
                lhsT=x_codes,
                lhsT_scale=x_plane,
                rhs=w_codes,
                rhs_scale=w_plane,
                start=(g == 0),
                stop=(g == PASSES - 1),
            )

        def home(half, c, t):
            rows = slice(t * P, (t + 1) * P)
            if c == VALUE_BLOCK:
                view = out_v[half, :, rows, :]
            elif c == KEY_BLOCK:
                view = out_k[half, :, rows, :]
            else:
                view = out_q[half, c, :, rows, :]
            return view.rearrange("h p d -> p h d")

        by_head = [P, HEADS, HEAD_DIM]
        waiting = []

        def finish_rope():
            for half, c, t, straight, crossed in waiting:
                result = results.tile([P, HEADS, HEAD_DIM], F32, name="result")
                nc.vector.tensor_tensor(
                    result[:].rearrange("p h (i j) -> p (h i) j", j=2),
                    straight[:].rearrange("p h (i j) -> p (h i) j", j=2),
                    crossed[:].rearrange("p h (i j) -> p (h i) j", j=2)[:, :, ::-1],
                    ALU.add,
                )
                nc.sync.dma_start(out=home(half, c, t), in_=result[:])
            waiting.clear()

        def epilogue(bank, half, c, t):
            values = bank[:].rearrange("p (h d) -> p h d", h=HEADS)
            if c == VALUE_BLOCK:
                finish_rope()
                result = results.tile([P, HEADS, HEAD_DIM], F32, name="result")
                nc.scalar.copy(result[:], values)
                nc.sync.dma_start(out=home(half, c, t), in_=result[:])
                return
            straight = work.tile([P, HEADS, HEAD_DIM], F32, name="straight")
            crossed = work.tile([P, HEADS, HEAD_DIM], F32, name="crossed")
            nc.vector.tensor_tensor(
                straight[:], values, cos_table[:, t, :].unsqueeze(1).to_broadcast(by_head), ALU.mult
            )
            nc.vector.tensor_tensor(
                crossed[:], values, sin_table[:, t, :].unsqueeze(1).to_broadcast(by_head), ALU.mult
            )
            finish_rope()
            waiting.append((half, c, t, straight, crossed))

        banks = []
        for t in range(TILES):
            bank = psum.tile([P, COLS], F32, name="bank")
            banks.append(bank)
        for g in range(EARLY):
            for t in range(TILES):
                multiply(banks[t], 0, 0, t, g)
        for t in range(TILES):
            for g in range(EARLY, PASSES):
                multiply(banks[t], 0, 0, t, g)
            epilogue(banks[t], 0, 0, t)

        for half in range(BATCH):
            for c in range(1 if half == 0 else 0, BLOCKS):
                for t in range(TILES):
                    if half == BATCH - 1 and c == BLOCKS - 1 and t == TILES - 1:
                        continue
                    bank = psum.tile([P, COLS], F32, name="bank")
                    for g in range(PASSES):
                        multiply(bank, half, c, t, g)
                    epilogue(bank, half, c, t)

        half, c, t = BATCH - 1, BLOCKS - 1, TILES - 1
        for part in range(2):
            n0, n1 = part * COLS // 2, (part + 1) * COLS // 2
            bank = psum.tile([P, COLS], F32, name="bank")
            for g in range(PASSES):
                multiply(bank, half, c, t, g, n0, n1)
            result = results.tile([P, HEADS // 2, HEAD_DIM], F32, name="result_part")
            values = bank[:, 0 : COLS // 2].rearrange("p (h d) -> p h d", d=HEAD_DIM)
            if part == 0:
                nc.scalar.copy(result[:], values)
            else:
                nc.vector.tensor_copy(result[:], values)
            nc.sync.dma_start(out=home(half, c, t)[:, part * HEADS // 2 : (part + 1) * HEADS // 2, :], in_=result[:])
